import numpy as np
import ml_dtypes


def mxq(x, axis, fmt="e4m3"):
    dtype, down = {"e4m3": (ml_dtypes.float8_e4m3fn, 7), "e5m2": (ml_dtypes.float8_e5m2, 14)}[fmt]
    v = np.moveaxis(np.asarray(x, np.float32).astype(ml_dtypes.bfloat16).astype(np.float64), axis, -1)
    blocks = v.reshape(v.shape[:-1] + (-1, 32))
    amax = np.abs(blocks).max(-1, keepdims=True)
    byte = np.maximum(np.where(amax > 0, np.frexp(amax)[1] - 1 + 127, 0) - down, 1)
    scale = np.exp2(byte - 127.0)
    codes = (blocks / scale).astype(np.float32).astype(dtype).astype(np.float64)
    return np.moveaxis((codes * scale).reshape(v.shape), -1, axis)


WIDE = False


def mx_kscale(k):
    if not WIDE:
        return np.ones(k)
    levels = np.array([10, -10, 5, -5, 0])
    a = np.random.permutation(np.resize(levels, k // 512 * 4)).reshape(k // 512, 4)
    idx = np.arange(k)
    return np.exp2(a[idx // 512, idx % 128 // 32])


BF16 = ml_dtypes.bfloat16


def bf(x):
    return np.asarray(x, np.float32).astype(BF16)


def f64(x):
    return np.asarray(x).astype(np.float64)


B, E, D, H = 256, 8, 128, 1024


def swish(v):
    with np.errstate(over="ignore"):
        return v / (1.0 + np.exp(-v))


def setup_inputs():
    a = mx_kscale(H)
    t = np.maximum(a, 1.0 / a) ** 2
    return {"u": bf(np.random.standard_normal((B * E, D))),
            "W1": bf(np.random.standard_normal((E, D, H)) * 1.5 / np.sqrt(D) * t),
            "b1": bf(np.random.standard_normal((E, H)) * 0.3 * t),
            "W2": bf(np.random.standard_normal((E, H, H)) * 1.5 / np.sqrt(H) / t[:, None]),
            "b2": bf(np.random.standard_normal((E, H)) * 0.3)}


def reference(u, W1, b1, W2, b2):
    x = f64(u).reshape(-1, E, D).transpose(1, 0, 2)
    h1 = swish(x @ f64(W1) + f64(b1)[:, None, :])
    h2 = swish((mxq(h1, 2, "e4m3") @ mxq(f64(W2), 1, "e4m3")) + f64(b2)[:, None, :])
    return h2.transpose(1, 0, 2)

@@ -1,0 +1,230 @@
+from contextlib import ExitStack
+
+import concourse.mybir as mybir
+from concourse.masks import make_identity
+
+BF16 = mybir.dt.bfloat16
+F32 = mybir.dt.float32
+U32 = mybir.dt.uint32
+U8 = mybir.dt.uint8
+FP8X4 = mybir.dt.float8_e4m3fn_x4
+SILU = mybir.ActivationFunctionType.Silu
+
+P = 128
+PACK = 4
+ENVS = 8
+BATCH = 256
+D_IN = 128
+HIDDEN = 1024
+K_PASS = P * PACK
+PASSES = HIDDEN // K_PASS
+ROW_SETS = BATCH // P
+HALF = 512
+HALVES = HIDDEN // HALF
+BLOCKS = HIDDEN // P
+COLS = HALF // P
+STEPS = ENVS * HALVES
+RUN = 4
+LOAD_AHEAD = 3
+
+FLOPS = 2 * ENVS * BATCH * HIDDEN * (D_IN + HIDDEN)
+
+
+def tile_environvectorfield_pa_kernel(tc, u, W1, b1, W2, b2, out):
+    nc = tc.nc
+    with ExitStack() as ctx:
+        const = ctx.enter_context(tc.tile_pool(name="const", bufs=1))
+        raw_pool = ctx.enter_context(tc.tile_pool(name="raw", bufs=LOAD_AHEAD * PASSES))
+        grouped_pool = ctx.enter_context(tc.tile_pool(name="grouped", bufs=4))
+        w2_mx_pool = ctx.enter_context(tc.tile_pool(name="w2_mx", bufs=3))
+        h1_pool = ctx.enter_context(tc.tile_pool(name="h1", bufs=3))
+        h1_mx_pool = ctx.enter_context(tc.tile_pool(name="h1_mx", bufs=3))
+        h2_pool = ctx.enter_context(tc.tile_pool(name="h2", bufs=3))
+        psum_setup = ctx.enter_context(tc.psum_pool(name="psum_setup", bufs=2))
+        psum_hidden = ctx.enter_context(tc.psum_pool(name="psum_hidden", bufs=2))
+        psum_mx = ctx.enter_context(tc.psum_pool(name="psum_mx", bufs=2))
+        psum_back = ctx.enter_context(tc.psum_pool(name="psum_back", bufs=2))
+
+        w1_sb = const.tile([P, ENVS, HIDDEN], BF16, name="w1_sb")
+        w2_raw = {}
+
+        def load_w2(e, c):
+            w2_raw[e, c] = raw_pool.tile([P, PACK, HIDDEN], BF16, name="w2_raw")
+            rows = W2[e, c * K_PASS : (c + 1) * K_PASS, :]
+            nc.sync.dma_start(out=w2_raw[e, c][:], in_=rows.rearrange("(t p) n -> p t n", p=P))
+
+        def load_weights(e):
+            nc.sync.dma_start(out=w1_sb[:, e, :], in_=W1[e])
+            for c in range(PASSES):
+                load_w2(e, c)
+
+        load_w2(0, 0)
+        u_sb = const.tile([P, ROW_SETS * ENVS, D_IN], BF16, name="u_sb")
+        nc.sync.dma_start(out=u_sb[:], in_=u.rearrange("(p i) d -> p i d", p=P))
+        bias_rows = const.tile([P, P], BF16, name="bias_rows")
+        nc.sync.dma_start(out=bias_rows[0 : ENVS * BLOCKS, :], in_=b1.rearrange("e (j p) -> (e j) p", p=P))
+        nc.sync.dma_start(out=bias_rows[ENVS * BLOCKS : P, :], in_=b2.rearrange("e (j p) -> (e j) p", p=P))
+        nc.sync.dma_start(out=w1_sb[:, 0, :], in_=W1[0])
+        load_w2(0, 1)
+        for e in range(1, LOAD_AHEAD):
+            load_weights(e)
+
+        ident_bf16 = const.tile([P, P], BF16, name="ident_bf16")
+        make_identity(nc, ident_bf16[:])
+        ident_f32 = const.tile([P, P], F32, name="ident_f32")
+        make_identity(nc, ident_f32[:])
+
+        xT = const.tile([P, ENVS, ROW_SETS, P], BF16, name="xT")
+        for s in range(ROW_SETS):
+            xT_ps = psum_setup.tile([P, ENVS, P], BF16, name="xT_ps", tag="setup")
+            for e in range(ENVS):
+                nc.tensor.transpose(out=xT_ps[:, e, :], in_=u_sb[:, s * ENVS + e, :], identity=ident_bf16[:])
+            nc.scalar.copy(out=xT[:, :, s, :], in_=xT_ps[:])
+
+        bias_ps = psum_setup.tile([P, P], BF16, name="bias_ps", tag="setup")
+        nc.tensor.transpose(out=bias_ps[:], in_=bias_rows[:], identity=ident_bf16[:])
+        bias_cols = const.tile([P, P], F32, name="bias_cols")
+        nc.vector.tensor_copy(out=bias_cols[:], in_=bias_ps[:])
+
+        def regroup(dst, src):
+            nc.vector.tensor_copy(
+                out=dst.rearrange("p (k i) t -> p k t i", i=RUN),
+                in_=src.rearrange("p t (k i) -> p k t i", i=RUN),
+            )
+
+        h1_bf16 = {}
+        h1_grouped = {}
+        h1_codes = {}
+        h1_scales = {}
+
+        def first_layer(e, c):
+            h1_bf16[e, c] = h1_pool.tile([P, PACK, BATCH], BF16, name="h1_bf16")
+            x_cols = xT[:, e, :, :].rearrange("d s p -> d (s p)")
+            for pair in range(PACK // 2):
+                acc = psum_hidden.tile([P, 2, BATCH], F32, name="hidden_acc")
+                for j in range(2):
+                    block = c * PACK + pair * 2 + j
+                    nc.tensor.matmul(
+                        out=acc[:, j, :],
+                        lhsT=w1_sb[:, e, block * P : (block + 1) * P],
+                        rhs=x_cols,
+                        start=True,
+                        stop=True,
+                    )
+                for j in range(2):
+                    block = c * PACK + pair * 2 + j
+                    nc.scalar.activation(
+                        out=h1_bf16[e, c][:, pair * 2 + j, :],
+                        in_=acc[:, j, :],
+                        func=SILU,
+                        bias=bias_cols[:, e * BLOCKS + block : e * BLOCKS + block + 1],
+                    )
+
+        def regroup_h1(e, c):
+            h1_grouped[e, c] = h1_pool.tile([P, BATCH, PACK], BF16, name="h1_grouped", align_bytes=64)
+            regroup(h1_grouped[e, c][:], h1_bf16[e, c][:])
+
+        def quantise_h1(e, c):
+            if c == 0:
+                h1_codes[e] = h1_mx_pool.tile([P, PASSES, BATCH], U32, name="h1_codes", align_bytes=64)
+                h1_scales[e] = h1_mx_pool.tile([P, PASSES, BATCH], U8, name="h1_scales", align_bytes=64)
+            nc.vector.quantize_mx(
+                out=h1_codes[e][:, c, :].bitcast(FP8X4),
+                scales=h1_scales[e][:, c, :],
+                in_=h1_grouped[e, c][:].rearrange("p w t -> p (w t)"),
+            )
+
+        w2_grouped = {}
+        w2_codes = {}
+        w2_scales = {}
+
+        def regroup_w2(e, half, c):
+            w2_grouped[e, half, c] = grouped_pool.tile([P, HALF, PACK], BF16, name="w2_grouped", align_bytes=64)
+            regroup(
+                w2_grouped[e, half, c][:],
+                w2_raw[e, c][:, :, half * HALF : (half + 1) * HALF],
+            )
+
+        def quantise_w2(e, half, c):
+            if c == 0:
+                w2_codes[e, half] = w2_mx_pool.tile([P, PASSES, HALF], U32, name="w2_codes", align_bytes=64)
+                w2_scales[e, half] = w2_mx_pool.tile([P, PASSES, HALF], U8, name="w2_scales", align_bytes=64)
+            nc.vector.quantize_mx(
+                out=w2_codes[e, half][:, c, :].bitcast(FP8X4),
+                scales=w2_scales[e, half][:, c, :],
+                in_=w2_grouped[e, half, c][:].rearrange("p w t -> p (w t)"),
+            )
+
+        h2T = {}
+        h2_back = {}
+
+        def second_layer(e, half):
+            h2T[e, half] = h2_pool.tile([P, COLS, BATCH], F32, name="h2T")
+            for pair in range(COLS // 2):
+                acc = psum_mx.tile([P, 2, BATCH], F32, name="mx_acc")
+                for j in range(2):
+                    col = pair * 2 + j
+                    for c in range(PASSES):
+                        nc.tensor.matmul_mx(
+                            out=acc[:, j, :],
+                            lhsT=w2_codes[e, half][:, c, col * P : (col + 1) * P].bitcast(FP8X4),
+                            lhsT_scale=w2_scales[e, half][:, c, col * P : (col + 1) * P],
+                            rhs=h1_codes[e][:, c, :].bitcast(FP8X4),
+                            rhs_scale=h1_scales[e][:, c, :],
+                            start=(c == 0),
+                            stop=(c == PASSES - 1),
+                        )
+                for j in range(2):
+                    col = pair * 2 + j
+                    block = ENVS * BLOCKS + e * BLOCKS + half * COLS + col
+                    nc.scalar.activation(
+                        out=h2T[e, half][:, col, :],
+                        in_=acc[:, j, :],
+                        func=SILU,
+                        bias=bias_cols[:, block : block + 1],
+                    )
+
+        def transpose_back(e, half):
+            for s in range(ROW_SETS):
+                h2_back[e, half, s] = psum_back.tile([P, COLS, P], F32, name="h2_back")
+                for col in range(COLS):
+                    nc.tensor.transpose(
+                        out=h2_back[e, half, s][:, col, :],
+                        in_=h2T[e, half][:, col, s * P : (s + 1) * P],
+                        identity=ident_f32[:],
+                    )
+
+        out_rows = out.rearrange("(p s) e n -> p s e n", s=ROW_SETS)
+
+        def store(e, half):
+            h2_sb = h2_pool.tile([P, ROW_SETS, HALF], F32, name="h2_sb")
+            for s in range(ROW_SETS):
+                nc.scalar.copy(out=h2_sb[:, s, :], in_=h2_back[e, half, s][:].rearrange("p c n -> p (c n)"))
+            nc.sync.dma_start(out=out_rows[:, :, e, half * HALF : (half + 1) * HALF], in_=h2_sb[:])
+
+        for first in range(2):
+            first_layer(*divmod(first, PASSES))
+        regroup_h1(0, 0)
+        quantise_h1(0, 0)
+
+        for i in range(STEPS + 2):
+            if i < STEPS:
+                e, half = divmod(i, HALVES)
+                if i + 1 < STEPS:
+                    regroup_h1(*divmod(i + 1, PASSES))
+                regroup_w2(e, half, 0)
+                if i + 1 < STEPS:
+                    quantise_h1(*divmod(i + 1, PASSES))
+                regroup_w2(e, half, 1)
+                quantise_w2(e, half, 0)
+                quantise_w2(e, half, 1)
+                if half == HALVES - 1 and e + LOAD_AHEAD < ENVS:
+                    load_weights(e + LOAD_AHEAD)
+            if 0 <= i - 2:
+                store(*divmod(i - 2, HALVES))
+            if 0 <= i - 1 < STEPS:
+                second_layer(*divmod(i - 1, HALVES))
+            if i + 2 < STEPS:
+                first_layer(*divmod(i + 2, PASSES))
+            if 0 <= i - 1 < STEPS:
+                transpose_back(*divmod(i - 1, HALVES))

@@ -26,6 +26,8 @@ COLS = HALF // P
 STEPS = ENVS * HALVES
 RUN = 4
 LOAD_AHEAD = 3
+ENVS_IN_BANK = 4
+FIRST_AHEAD = 2
 
 FLOPS = 2 * ENVS * BATCH * HIDDEN * (D_IN + HIDDEN)
 
@@ -40,10 +42,12 @@ def tile_environvectorfield_pa_kernel(tc, u, W1, b1, W2, b2, out):
         h1_pool = ctx.enter_context(tc.tile_pool(name="h1", bufs=3))
         h1_mx_pool = ctx.enter_context(tc.tile_pool(name="h1_mx", bufs=3))
         h2_pool = ctx.enter_context(tc.tile_pool(name="h2", bufs=3))
+        out_pool = ctx.enter_context(tc.tile_pool(name="out", bufs=4))
         psum_setup = ctx.enter_context(tc.psum_pool(name="psum_setup", bufs=2))
         psum_hidden = ctx.enter_context(tc.psum_pool(name="psum_hidden", bufs=2))
         psum_mx = ctx.enter_context(tc.psum_pool(name="psum_mx", bufs=2))
         psum_back = ctx.enter_context(tc.psum_pool(name="psum_back", bufs=2))
+        ctx.enter_context(tc.manual_schedule())
 
         w1_sb = const.tile([P, ENVS, HIDDEN], BF16, name="w1_sb")
         w2_raw = {}
@@ -75,19 +79,22 @@ def tile_environvectorfield_pa_kernel(tc, u, W1, b1, W2, b2, out):
         make_identity(nc, ident_f32[:])
 
         xT = const.tile([P, ENVS, ROW_SETS, P], BF16, name="xT")
-        for s in range(ROW_SETS):
-            xT_ps = psum_setup.tile([P, ENVS, P], BF16, name="xT_ps", tag="setup")
-            for e in range(ENVS):
-                nc.tensor.transpose(out=xT_ps[:, e, :], in_=u_sb[:, s * ENVS + e, :], identity=ident_bf16[:])
-            nc.scalar.copy(out=xT[:, :, s, :], in_=xT_ps[:])
+        for e0 in range(0, ENVS, ENVS_IN_BANK):
+            xT_ps = psum_setup.tile([P, ENVS_IN_BANK, ROW_SETS, P], BF16, name="xT_ps", tag="setup")
+            for e in range(ENVS_IN_BANK):
+                for s in range(ROW_SETS):
+                    nc.tensor.transpose(
+                        out=xT_ps[:, e, s, :], in_=u_sb[:, s * ENVS + e0 + e, :], identity=ident_bf16[:]
+                    )
+            nc.scalar.copy(out=xT[:, e0 : e0 + ENVS_IN_BANK, :, :], in_=xT_ps[:])
 
         bias_ps = psum_setup.tile([P, P], BF16, name="bias_ps", tag="setup")
         nc.tensor.transpose(out=bias_ps[:], in_=bias_rows[:], identity=ident_bf16[:])
         bias_cols = const.tile([P, P], F32, name="bias_cols")
-        nc.vector.tensor_copy(out=bias_cols[:], in_=bias_ps[:])
+        nc.scalar.copy(out=bias_cols[:], in_=bias_ps[:])
 
-        def regroup(dst, src):
-            nc.vector.tensor_copy(
+        def regroup(copy, dst, src):
+            copy(
                 out=dst.rearrange("p (k i) t -> p k t i", i=RUN),
                 in_=src.rearrange("p t (k i) -> p k t i", i=RUN),
             )
@@ -122,7 +129,8 @@ def tile_environvectorfield_pa_kernel(tc, u, W1, b1, W2, b2, out):
 
         def regroup_h1(e, c):
             h1_grouped[e, c] = h1_pool.tile([P, BATCH, PACK], BF16, name="h1_grouped", align_bytes=64)
-            regroup(h1_grouped[e, c][:], h1_bf16[e, c][:])
+            copy = nc.scalar.copy if c == PASSES - 1 else nc.vector.tensor_copy
+            regroup(copy, h1_grouped[e, c][:], h1_bf16[e, c][:])
 
         def quantise_h1(e, c):
             if c == 0:
@@ -141,6 +149,7 @@ def tile_environvectorfield_pa_kernel(tc, u, W1, b1, W2, b2, out):
         def regroup_w2(e, half, c):
             w2_grouped[e, half, c] = grouped_pool.tile([P, HALF, PACK], BF16, name="w2_grouped", align_bytes=64)
             regroup(
+                nc.vector.tensor_copy,
                 w2_grouped[e, half, c][:],
                 w2_raw[e, c][:, :, half * HALF : (half + 1) * HALF],
             )
@@ -187,7 +196,8 @@ def tile_environvectorfield_pa_kernel(tc, u, W1, b1, W2, b2, out):
         def transpose_back(e, half):
             for s in range(ROW_SETS):
                 h2_back[e, half, s] = psum_back.tile([P, COLS, P], F32, name="h2_back")
-                for col in range(COLS):
+            for col in range(COLS):
+                for s in range(ROW_SETS):
                     nc.tensor.transpose(
                         out=h2_back[e, half, s][:, col, :],
                         in_=h2T[e, half][:, col, s * P : (s + 1) * P],
@@ -197,34 +207,45 @@ def tile_environvectorfield_pa_kernel(tc, u, W1, b1, W2, b2, out):
         out_rows = out.rearrange("(p s) e n -> p s e n", s=ROW_SETS)
 
         def store(e, half):
-            h2_sb = h2_pool.tile([P, ROW_SETS, HALF], F32, name="h2_sb")
             for s in range(ROW_SETS):
-                nc.scalar.copy(out=h2_sb[:, s, :], in_=h2_back[e, half, s][:].rearrange("p c n -> p (c n)"))
-            nc.sync.dma_start(out=out_rows[:, :, e, half * HALF : (half + 1) * HALF], in_=h2_sb[:])
+                h2_sb = out_pool.tile([P, HALF], F32, name="h2_sb")
+                nc.scalar.copy(out=h2_sb[:], in_=h2_back[e, half, s][:].rearrange("p c n -> p (c n)"))
+                nc.sync.dma_start(out=out_rows[:, s, e, half * HALF : (half + 1) * HALF], in_=h2_sb[:])
 
-        for first in range(2):
+        def vector_round(i):
+            e, half = divmod(i, HALVES)
+            regroup_w2(e, half, 0)
+            regroup_w2(e, half, 1)
+            quantise_w2(e, half, 0)
+            if i + 1 < STEPS:
+                regroup_h1(*divmod(i + 1, PASSES))
+            quantise_w2(e, half, 1)
+            if i + 1 < STEPS:
+                quantise_h1(*divmod(i + 1, PASSES))
+
+        for c in range(PASSES):
+            for half in range(HALVES):
+                regroup_w2(0, half, c)
+            for half in range(HALVES):
+                quantise_w2(0, half, c)
+        load_weights(LOAD_AHEAD)
+        for first in range(FIRST_AHEAD + 1):
             first_layer(*divmod(first, PASSES))
-        regroup_h1(0, 0)
-        quantise_h1(0, 0)
+            regroup_h1(*divmod(first, PASSES))
+        for first in range(FIRST_AHEAD + 1):
+            quantise_h1(*divmod(first, PASSES))
 
-        for i in range(STEPS + 2):
-            if i < STEPS:
-                e, half = divmod(i, HALVES)
-                if i + 1 < STEPS:
-                    regroup_h1(*divmod(i + 1, PASSES))
-                regroup_w2(e, half, 0)
-                if i + 1 < STEPS:
-                    quantise_h1(*divmod(i + 1, PASSES))
-                regroup_w2(e, half, 1)
-                quantise_w2(e, half, 0)
-                quantise_w2(e, half, 1)
-                if half == HALVES - 1 and e + LOAD_AHEAD < ENVS:
-                    load_weights(e + LOAD_AHEAD)
+        for i in range(1, STEPS + 2):
             if 0 <= i - 2:
                 store(*divmod(i - 2, HALVES))
-            if 0 <= i - 1 < STEPS:
+            if HALVES <= i < STEPS:
+                vector_round(i)
+                e, half = divmod(i, HALVES)
+                if half == HALVES - 1 and e + LOAD_AHEAD < ENVS:
+                    load_weights(e + LOAD_AHEAD)
+            if i - 1 < STEPS:
                 second_layer(*divmod(i - 1, HALVES))
-            if i + 2 < STEPS:
-                first_layer(*divmod(i + 2, PASSES))
-            if 0 <= i - 1 < STEPS:
+            if i + FIRST_AHEAD < STEPS:
+                first_layer(*divmod(i + FIRST_AHEAD, PASSES))
+            if i - 1 < STEPS:
                 transpose_back(*divmod(i - 1, HALVES))

@@ -18,16 +18,17 @@ D_IN = 128
 HIDDEN = 1024
 K_PASS = P * PACK
 PASSES = HIDDEN // K_PASS
+BLOCKS = HIDDEN // P
 ROW_SETS = BATCH // P
 HALF = 512
 HALVES = HIDDEN // HALF
-BLOCKS = HIDDEN // P
 COLS = HALF // P
 STEPS = ENVS * HALVES
 RUN = 4
 LOAD_AHEAD = 3
-ENVS_IN_BANK = 4
 FIRST_AHEAD = 2
+ENVS_IN_BANK = 4
+H1_SCALAR_COLS = 128
 
 FLOPS = 2 * ENVS * BATCH * HIDDEN * (D_IN + HIDDEN)
 
@@ -36,8 +37,8 @@ def tile_environvectorfield_pa_kernel(tc, u, W1, b1, W2, b2, out):
     nc = tc.nc
     with ExitStack() as ctx:
         const = ctx.enter_context(tc.tile_pool(name="const", bufs=1))
-        raw_pool = ctx.enter_context(tc.tile_pool(name="raw", bufs=LOAD_AHEAD * PASSES))
-        grouped_pool = ctx.enter_context(tc.tile_pool(name="grouped", bufs=4))
+        raw_pool = ctx.enter_context(tc.tile_pool(name="raw", bufs=LOAD_AHEAD))
+        grouped_pool = ctx.enter_context(tc.tile_pool(name="grouped", bufs=3))
         w2_mx_pool = ctx.enter_context(tc.tile_pool(name="w2_mx", bufs=3))
         h1_pool = ctx.enter_context(tc.tile_pool(name="h1", bufs=3))
         h1_mx_pool = ctx.enter_context(tc.tile_pool(name="h1_mx", bufs=3))
@@ -47,28 +48,31 @@ def tile_environvectorfield_pa_kernel(tc, u, W1, b1, W2, b2, out):
         psum_hidden = ctx.enter_context(tc.psum_pool(name="psum_hidden", bufs=2))
         psum_mx = ctx.enter_context(tc.psum_pool(name="psum_mx", bufs=2))
         psum_back = ctx.enter_context(tc.psum_pool(name="psum_back", bufs=2))
-        ctx.enter_context(tc.manual_schedule())
 
         w1_sb = const.tile([P, ENVS, HIDDEN], BF16, name="w1_sb")
         w2_raw = {}
 
+        def load_w1(e):
+            nc.sync.dma_start(out=w1_sb[:, e, :], in_=W1[e])
+
         def load_w2(e, c):
-            w2_raw[e, c] = raw_pool.tile([P, PACK, HIDDEN], BF16, name="w2_raw")
+            if c == 0:
+                w2_raw[e] = raw_pool.tile([P, PASSES, PACK, HIDDEN], BF16, name="w2_raw")
             rows = W2[e, c * K_PASS : (c + 1) * K_PASS, :]
-            nc.sync.dma_start(out=w2_raw[e, c][:], in_=rows.rearrange("(t p) n -> p t n", p=P))
+            nc.sync.dma_start(out=w2_raw[e][:, c, :, :], in_=rows.rearrange("(t p) n -> p t n", p=P))
 
         def load_weights(e):
-            nc.sync.dma_start(out=w1_sb[:, e, :], in_=W1[e])
+            load_w1(e)
             for c in range(PASSES):
                 load_w2(e, c)
 
         load_w2(0, 0)
-        u_sb = const.tile([P, ROW_SETS * ENVS, D_IN], BF16, name="u_sb")
-        nc.sync.dma_start(out=u_sb[:], in_=u.rearrange("(p i) d -> p i d", p=P))
         bias_rows = const.tile([P, P], BF16, name="bias_rows")
         nc.sync.dma_start(out=bias_rows[0 : ENVS * BLOCKS, :], in_=b1.rearrange("e (j p) -> (e j) p", p=P))
         nc.sync.dma_start(out=bias_rows[ENVS * BLOCKS : P, :], in_=b2.rearrange("e (j p) -> (e j) p", p=P))
-        nc.sync.dma_start(out=w1_sb[:, 0, :], in_=W1[0])
+        u_sb = const.tile([P, ROW_SETS * ENVS, D_IN], BF16, name="u_sb")
+        nc.sync.dma_start(out=u_sb[:], in_=u.rearrange("(p i) d -> p i d", p=P))
+        load_w1(0)
         load_w2(0, 1)
         for e in range(1, LOAD_AHEAD):
             load_weights(e)
@@ -78,8 +82,14 @@ def tile_environvectorfield_pa_kernel(tc, u, W1, b1, W2, b2, out):
         ident_f32 = const.tile([P, P], F32, name="ident_f32")
         make_identity(nc, ident_f32[:])
 
+        bias_ps = psum_setup.tile([P, P], BF16, name="bias_ps", tag="setup")
+        nc.tensor.transpose(out=bias_ps[:], in_=bias_rows[:], identity=ident_bf16[:])
+        bias_cols = const.tile([P, P], F32, name="bias_cols")
+        nc.scalar.copy(out=bias_cols[:], in_=bias_ps[:])
+
         xT = const.tile([P, ENVS, ROW_SETS, P], BF16, name="xT")
-        for e0 in range(0, ENVS, ENVS_IN_BANK):
+
+        def transpose_x(e0):
             xT_ps = psum_setup.tile([P, ENVS_IN_BANK, ROW_SETS, P], BF16, name="xT_ps", tag="setup")
             for e in range(ENVS_IN_BANK):
                 for s in range(ROW_SETS):
@@ -87,17 +97,6 @@ def tile_environvectorfield_pa_kernel(tc, u, W1, b1, W2, b2, out):
                         out=xT_ps[:, e, s, :], in_=u_sb[:, s * ENVS + e0 + e, :], identity=ident_bf16[:]
                     )
             nc.scalar.copy(out=xT[:, e0 : e0 + ENVS_IN_BANK, :, :], in_=xT_ps[:])
-
-        bias_ps = psum_setup.tile([P, P], BF16, name="bias_ps", tag="setup")
-        nc.tensor.transpose(out=bias_ps[:], in_=bias_rows[:], identity=ident_bf16[:])
-        bias_cols = const.tile([P, P], F32, name="bias_cols")
-        nc.scalar.copy(out=bias_cols[:], in_=bias_ps[:])
-
-        def regroup(copy, dst, src):
-            copy(
-                out=dst.rearrange("p (k i) t -> p k t i", i=RUN),
-                in_=src.rearrange("p t (k i) -> p k t i", i=RUN),
-            )
 
         h1_bf16 = {}
         h1_grouped = {}
@@ -129,8 +128,15 @@ def tile_environvectorfield_pa_kernel(tc, u, W1, b1, W2, b2, out):
 
         def regroup_h1(e, c):
             h1_grouped[e, c] = h1_pool.tile([P, BATCH, PACK], BF16, name="h1_grouped", align_bytes=64)
-            copy = nc.scalar.copy if c == PASSES - 1 else nc.vector.tensor_copy
-            regroup(copy, h1_grouped[e, c][:], h1_bf16[e, c][:])
+            split = BATCH - H1_SCALAR_COLS
+            nc.vector.tensor_copy(
+                out=h1_grouped[e, c][:, 0:split, :].rearrange("p (k i) t -> p k t i", i=RUN),
+                in_=h1_bf16[e, c][:, :, 0:split].rearrange("p t (k i) -> p k t i", i=RUN),
+            )
+            nc.scalar.copy(
+                out=h1_grouped[e, c][:, split:BATCH, :].rearrange("p (k i) t -> p k t i", i=RUN),
+                in_=h1_bf16[e, c][:, :, split:BATCH].rearrange("p t (k i) -> p k t i", i=RUN),
+            )
 
         def quantise_h1(e, c):
             if c == 0:
@@ -146,22 +152,26 @@ def tile_environvectorfield_pa_kernel(tc, u, W1, b1, W2, b2, out):
         w2_codes = {}
         w2_scales = {}
 
-        def regroup_w2(e, half, c):
-            w2_grouped[e, half, c] = grouped_pool.tile([P, HALF, PACK], BF16, name="w2_grouped", align_bytes=64)
-            regroup(
-                nc.vector.tensor_copy,
-                w2_grouped[e, half, c][:],
-                w2_raw[e, c][:, :, half * HALF : (half + 1) * HALF],
+        def regroup_w2(e, half, c0, c1):
+            if c0 == 0:
+                w2_grouped[e, half] = grouped_pool.tile(
+                    [P, PASSES, HALF, PACK], BF16, name="w2_grouped", align_bytes=64
+                )
+            nc.vector.tensor_copy(
+                out=w2_grouped[e, half][:, c0:c1, :, :].rearrange("p c (k i) t -> p c k t i", i=RUN),
+                in_=w2_raw[e][:, c0:c1, :, half * HALF : (half + 1) * HALF].rearrange(
+                    "p c t (k i) -> p c k t i", i=RUN
+                ),
             )
 
-        def quantise_w2(e, half, c):
-            if c == 0:
+        def quantise_w2(e, half, c0, c1):
+            if c0 == 0:
                 w2_codes[e, half] = w2_mx_pool.tile([P, PASSES, HALF], U32, name="w2_codes", align_bytes=64)
                 w2_scales[e, half] = w2_mx_pool.tile([P, PASSES, HALF], U8, name="w2_scales", align_bytes=64)
             nc.vector.quantize_mx(
-                out=w2_codes[e, half][:, c, :].bitcast(FP8X4),
-                scales=w2_scales[e, half][:, c, :],
-                in_=w2_grouped[e, half, c][:].rearrange("p w t -> p (w t)"),
+                out=w2_codes[e, half][:, c0:c1, :].rearrange("p c w -> p (c w)").bitcast(FP8X4),
+                scales=w2_scales[e, half][:, c0:c1, :].rearrange("p c w -> p (c w)"),
+                in_=w2_grouped[e, half][:, c0:c1, :, :].rearrange("p c w t -> p (c w t)"),
             )
 
         h2T = {}
@@ -206,41 +216,38 @@ def tile_environvectorfield_pa_kernel(tc, u, W1, b1, W2, b2, out):
 
         out_rows = out.rearrange("(p s) e n -> p s e n", s=ROW_SETS)
 
-        def store(e, half):
+        def store(e, half, vector_is_free):
             for s in range(ROW_SETS):
                 h2_sb = out_pool.tile([P, HALF], F32, name="h2_sb")
-                nc.scalar.copy(out=h2_sb[:], in_=h2_back[e, half, s][:].rearrange("p c n -> p (c n)"))
+                copy = nc.vector.tensor_copy if vector_is_free and s == ROW_SETS - 1 else nc.scalar.copy
+                copy(out=h2_sb[:], in_=h2_back[e, half, s][:].rearrange("p c n -> p (c n)"))
                 nc.sync.dma_start(out=out_rows[:, s, e, half * HALF : (half + 1) * HALF], in_=h2_sb[:])
-
-        def vector_round(i):
-            e, half = divmod(i, HALVES)
-            regroup_w2(e, half, 0)
-            regroup_w2(e, half, 1)
-            quantise_w2(e, half, 0)
-            if i + 1 < STEPS:
-                regroup_h1(*divmod(i + 1, PASSES))
-            quantise_w2(e, half, 1)
-            if i + 1 < STEPS:
-                quantise_h1(*divmod(i + 1, PASSES))
 
         for c in range(PASSES):
             for half in range(HALVES):
-                regroup_w2(0, half, c)
+                regroup_w2(0, half, c, c + 1)
             for half in range(HALVES):
-                quantise_w2(0, half, c)
+                quantise_w2(0, half, c, c + 1)
         load_weights(LOAD_AHEAD)
+        transpose_x(0)
         for first in range(FIRST_AHEAD + 1):
             first_layer(*divmod(first, PASSES))
             regroup_h1(*divmod(first, PASSES))
+        transpose_x(ENVS_IN_BANK)
         for first in range(FIRST_AHEAD + 1):
             quantise_h1(*divmod(first, PASSES))
 
         for i in range(1, STEPS + 2):
             if 0 <= i - 2:
-                store(*divmod(i - 2, HALVES))
+                store(*divmod(i - 2, HALVES), vector_is_free=(i >= STEPS))
             if HALVES <= i < STEPS:
-                vector_round(i)
                 e, half = divmod(i, HALVES)
+                regroup_w2(e, half, 0, PASSES)
+                if i + 1 < STEPS:
+                    regroup_h1(*divmod(i + 1, PASSES))
+                quantise_w2(e, half, 0, PASSES)
+                if i + 1 < STEPS:
+                    quantise_h1(*divmod(i + 1, PASSES))
                 if half == HALVES - 1 and e + LOAD_AHEAD < ENVS:
                     load_weights(e + LOAD_AHEAD)
             if i - 1 < STEPS:

@@ -48,6 +48,7 @@ def tile_environvectorfield_pa_kernel(tc, u, W1, b1, W2, b2, out):
         psum_hidden = ctx.enter_context(tc.psum_pool(name="psum_hidden", bufs=2))
         psum_mx = ctx.enter_context(tc.psum_pool(name="psum_mx", bufs=2))
         psum_back = ctx.enter_context(tc.psum_pool(name="psum_back", bufs=2))
+        ctx.enter_context(tc.manual_schedule())
 
         w1_sb = const.tile([P, ENVS, HIDDEN], BF16, name="w1_sb")
         w2_raw = {}

@@ -18,17 +18,22 @@ D_IN = 128
 HIDDEN = 1024
 K_PASS = P * PACK
 PASSES = HIDDEN // K_PASS
-BLOCKS = HIDDEN // P
+CHUNKS = HIDDEN // P
 ROW_SETS = BATCH // P
-HALF = 512
+BANK = 512
+GROUPS_IN_BANK = BANK // BATCH
+ENVS_IN_BANK = 4
+
+HALF = BANK
 HALVES = HIDDEN // HALF
 COLS = HALF // P
 STEPS = ENVS * HALVES
+
 RUN = 4
 LOAD_AHEAD = 3
 FIRST_AHEAD = 2
-ENVS_IN_BANK = 4
-H1_SCALAR_COLS = 128
+HAND_OVER = 3
+H1_SCALAR_COLS = 64
 
 FLOPS = 2 * ENVS * BATCH * HIDDEN * (D_IN + HIDDEN)
 
@@ -38,12 +43,12 @@ def tile_environvectorfield_pa_kernel(tc, u, W1, b1, W2, b2, out):
     with ExitStack() as ctx:
         const = ctx.enter_context(tc.tile_pool(name="const", bufs=1))
         raw_pool = ctx.enter_context(tc.tile_pool(name="raw", bufs=LOAD_AHEAD))
-        grouped_pool = ctx.enter_context(tc.tile_pool(name="grouped", bufs=3))
-        w2_mx_pool = ctx.enter_context(tc.tile_pool(name="w2_mx", bufs=3))
-        h1_pool = ctx.enter_context(tc.tile_pool(name="h1", bufs=3))
-        h1_mx_pool = ctx.enter_context(tc.tile_pool(name="h1_mx", bufs=3))
-        h2_pool = ctx.enter_context(tc.tile_pool(name="h2", bufs=3))
-        out_pool = ctx.enter_context(tc.tile_pool(name="out", bufs=4))
+        grouped_pool = ctx.enter_context(tc.tile_pool(name="grouped", bufs=HAND_OVER))
+        w2_mx_pool = ctx.enter_context(tc.tile_pool(name="w2_mx", bufs=HAND_OVER))
+        h1_pool = ctx.enter_context(tc.tile_pool(name="h1", bufs=HAND_OVER))
+        h1_mx_pool = ctx.enter_context(tc.tile_pool(name="h1_mx", bufs=HAND_OVER))
+        h2_pool = ctx.enter_context(tc.tile_pool(name="h2", bufs=HAND_OVER))
+        out_pool = ctx.enter_context(tc.tile_pool(name="out", bufs=2 * ROW_SETS))
         psum_setup = ctx.enter_context(tc.psum_pool(name="psum_setup", bufs=2))
         psum_hidden = ctx.enter_context(tc.psum_pool(name="psum_hidden", bufs=2))
         psum_mx = ctx.enter_context(tc.psum_pool(name="psum_mx", bufs=2))
@@ -69,8 +74,8 @@ def tile_environvectorfield_pa_kernel(tc, u, W1, b1, W2, b2, out):
 
         load_w2(0, 0)
         bias_rows = const.tile([P, P], BF16, name="bias_rows")
-        nc.sync.dma_start(out=bias_rows[0 : ENVS * BLOCKS, :], in_=b1.rearrange("e (j p) -> (e j) p", p=P))
-        nc.sync.dma_start(out=bias_rows[ENVS * BLOCKS : P, :], in_=b2.rearrange("e (j p) -> (e j) p", p=P))
+        nc.sync.dma_start(out=bias_rows[0 : ENVS * CHUNKS, :], in_=b1.rearrange("e (j p) -> (e j) p", p=P))
+        nc.sync.dma_start(out=bias_rows[ENVS * CHUNKS : P, :], in_=b2.rearrange("e (j p) -> (e j) p", p=P))
         u_sb = const.tile([P, ROW_SETS * ENVS, D_IN], BF16, name="u_sb")
         nc.sync.dma_start(out=u_sb[:], in_=u.rearrange("(p i) d -> p i d", p=P))
         load_w1(0)
@@ -107,24 +112,24 @@ def tile_environvectorfield_pa_kernel(tc, u, W1, b1, W2, b2, out):
         def first_layer(e, c):
             h1_bf16[e, c] = h1_pool.tile([P, PACK, BATCH], BF16, name="h1_bf16")
             x_cols = xT[:, e, :, :].rearrange("d s p -> d (s p)")
-            for pair in range(PACK // 2):
-                acc = psum_hidden.tile([P, 2, BATCH], F32, name="hidden_acc")
-                for j in range(2):
-                    block = c * PACK + pair * 2 + j
+            for bank in range(PACK // GROUPS_IN_BANK):
+                acc = psum_hidden.tile([P, GROUPS_IN_BANK, BATCH], F32, name="hidden_acc")
+                for j in range(GROUPS_IN_BANK):
+                    chunk = c * PACK + bank * GROUPS_IN_BANK + j
                     nc.tensor.matmul(
                         out=acc[:, j, :],
-                        lhsT=w1_sb[:, e, block * P : (block + 1) * P],
+                        lhsT=w1_sb[:, e, chunk * P : (chunk + 1) * P],
                         rhs=x_cols,
                         start=True,
                         stop=True,
                     )
-                for j in range(2):
-                    block = c * PACK + pair * 2 + j
+                for j in range(GROUPS_IN_BANK):
+                    chunk = c * PACK + bank * GROUPS_IN_BANK + j
                     nc.scalar.activation(
-                        out=h1_bf16[e, c][:, pair * 2 + j, :],
+                        out=h1_bf16[e, c][:, bank * GROUPS_IN_BANK + j, :],
                         in_=acc[:, j, :],
                         func=SILU,
-                        bias=bias_cols[:, e * BLOCKS + block : e * BLOCKS + block + 1],
+                        bias=bias_cols[:, e * CHUNKS + chunk : e * CHUNKS + chunk + 1],
                     )
 
         def regroup_h1(e, c):
@@ -180,10 +185,10 @@ def tile_environvectorfield_pa_kernel(tc, u, W1, b1, W2, b2, out):
 
         def second_layer(e, half):
             h2T[e, half] = h2_pool.tile([P, COLS, BATCH], F32, name="h2T")
-            for pair in range(COLS // 2):
-                acc = psum_mx.tile([P, 2, BATCH], F32, name="mx_acc")
-                for j in range(2):
-                    col = pair * 2 + j
+            for bank in range(COLS // GROUPS_IN_BANK):
+                acc = psum_mx.tile([P, GROUPS_IN_BANK, BATCH], F32, name="mx_acc")
+                for j in range(GROUPS_IN_BANK):
+                    col = bank * GROUPS_IN_BANK + j
                     for c in range(PASSES):
                         nc.tensor.matmul_mx(
                             out=acc[:, j, :],
@@ -194,14 +199,14 @@ def tile_environvectorfield_pa_kernel(tc, u, W1, b1, W2, b2, out):
                             start=(c == 0),
                             stop=(c == PASSES - 1),
                         )
-                for j in range(2):
-                    col = pair * 2 + j
-                    block = ENVS * BLOCKS + e * BLOCKS + half * COLS + col
+                for j in range(GROUPS_IN_BANK):
+                    col = bank * GROUPS_IN_BANK + j
+                    b2_col = ENVS * CHUNKS + e * CHUNKS + half * COLS + col
                     nc.scalar.activation(
                         out=h2T[e, half][:, col, :],
                         in_=acc[:, j, :],
                         func=SILU,
-                        bias=bias_cols[:, block : block + 1],
+                        bias=bias_cols[:, b2_col : b2_col + 1],
                     )
 
         def transpose_back(e, half):
@@ -231,12 +236,12 @@ def tile_environvectorfield_pa_kernel(tc, u, W1, b1, W2, b2, out):
                 quantise_w2(0, half, c, c + 1)
         load_weights(LOAD_AHEAD)
         transpose_x(0)
-        for first in range(FIRST_AHEAD + 1):
-            first_layer(*divmod(first, PASSES))
-            regroup_h1(*divmod(first, PASSES))
+        for step in range(FIRST_AHEAD + 1):
+            first_layer(*divmod(step, PASSES))
+            regroup_h1(*divmod(step, PASSES))
         transpose_x(ENVS_IN_BANK)
-        for first in range(FIRST_AHEAD + 1):
-            quantise_h1(*divmod(first, PASSES))
+        for step in range(FIRST_AHEAD + 1):
+            quantise_h1(*divmod(step, PASSES))
 
         for i in range(1, STEPS + 2):
             if 0 <= i - 2:

from contextlib import ExitStack

import concourse.mybir as mybir
from concourse.masks import make_identity

BF16 = mybir.dt.bfloat16
F32 = mybir.dt.float32
U32 = mybir.dt.uint32
U8 = mybir.dt.uint8
FP8X4 = mybir.dt.float8_e4m3fn_x4
SILU = mybir.ActivationFunctionType.Silu

P = 128
PACK = 4
ENVS = 8
BATCH = 256
D_IN = 128
HIDDEN = 1024
K_PASS = P * PACK
PASSES = HIDDEN // K_PASS
CHUNKS = HIDDEN // P
ROW_SETS = BATCH // P
BANK = 512
GROUPS_IN_BANK = BANK // BATCH
ENVS_IN_BANK = 4

HALF = BANK
HALVES = HIDDEN // HALF
COLS = HALF // P
STEPS = ENVS * HALVES

RUN = 4
LOAD_AHEAD = 3
FIRST_AHEAD = 2
HAND_OVER = 3
H1_SCALAR_COLS = 64

FLOPS = 2 * ENVS * BATCH * HIDDEN * (D_IN + HIDDEN)


def tile_environvectorfield_pa_kernel(tc, u, W1, b1, W2, b2, out):
    nc = tc.nc
    with ExitStack() as ctx:
        const = ctx.enter_context(tc.tile_pool(name="const", bufs=1))
        raw_pool = ctx.enter_context(tc.tile_pool(name="raw", bufs=LOAD_AHEAD))
        grouped_pool = ctx.enter_context(tc.tile_pool(name="grouped", bufs=HAND_OVER))
        w2_mx_pool = ctx.enter_context(tc.tile_pool(name="w2_mx", bufs=HAND_OVER))
        h1_pool = ctx.enter_context(tc.tile_pool(name="h1", bufs=HAND_OVER))
        h1_mx_pool = ctx.enter_context(tc.tile_pool(name="h1_mx", bufs=HAND_OVER))
        h2_pool = ctx.enter_context(tc.tile_pool(name="h2", bufs=HAND_OVER))
        out_pool = ctx.enter_context(tc.tile_pool(name="out", bufs=2 * ROW_SETS))
        psum_setup = ctx.enter_context(tc.psum_pool(name="psum_setup", bufs=2))
        psum_hidden = ctx.enter_context(tc.psum_pool(name="psum_hidden", bufs=2))
        psum_mx = ctx.enter_context(tc.psum_pool(name="psum_mx", bufs=2))
        psum_back = ctx.enter_context(tc.psum_pool(name="psum_back", bufs=2))
        ctx.enter_context(tc.manual_schedule())

        w1_sb = const.tile([P, ENVS, HIDDEN], BF16, name="w1_sb")
        w2_raw = {}

        def load_w1(e):
            nc.sync.dma_start(out=w1_sb[:, e, :], in_=W1[e])

        def load_w2(e, c):
            if c == 0:
                w2_raw[e] = raw_pool.tile([P, PASSES, PACK, HIDDEN], BF16, name="w2_raw")
            rows = W2[e, c * K_PASS : (c + 1) * K_PASS, :]
            nc.sync.dma_start(out=w2_raw[e][:, c, :, :], in_=rows.rearrange("(t p) n -> p t n", p=P))

        def load_weights(e):
            load_w1(e)
            for c in range(PASSES):
                load_w2(e, c)

        load_w2(0, 0)
        bias_rows = const.tile([P, P], BF16, name="bias_rows")
        nc.sync.dma_start(out=bias_rows[0 : ENVS * CHUNKS, :], in_=b1.rearrange("e (j p) -> (e j) p", p=P))
        nc.sync.dma_start(out=bias_rows[ENVS * CHUNKS : P, :], in_=b2.rearrange("e (j p) -> (e j) p", p=P))
        u_sb = const.tile([P, ROW_SETS * ENVS, D_IN], BF16, name="u_sb")
        nc.sync.dma_start(out=u_sb[:], in_=u.rearrange("(p i) d -> p i d", p=P))
        load_w1(0)
        load_w2(0, 1)
        for e in range(1, LOAD_AHEAD):
            load_weights(e)

        ident_bf16 = const.tile([P, P], BF16, name="ident_bf16")
        make_identity(nc, ident_bf16[:])
        ident_f32 = const.tile([P, P], F32, name="ident_f32")
        make_identity(nc, ident_f32[:])

        bias_ps = psum_setup.tile([P, P], BF16, name="bias_ps", tag="setup")
        nc.tensor.transpose(out=bias_ps[:], in_=bias_rows[:], identity=ident_bf16[:])
        bias_cols = const.tile([P, P], F32, name="bias_cols")
        nc.scalar.copy(out=bias_cols[:], in_=bias_ps[:])

        xT = const.tile([P, ENVS, ROW_SETS, P], BF16, name="xT")

        def transpose_x(e0):
            xT_ps = psum_setup.tile([P, ENVS_IN_BANK, ROW_SETS, P], BF16, name="xT_ps", tag="setup")
            for e in range(ENVS_IN_BANK):
                for s in range(ROW_SETS):
                    nc.tensor.transpose(
                        out=xT_ps[:, e, s, :], in_=u_sb[:, s * ENVS + e0 + e, :], identity=ident_bf16[:]
                    )
            nc.scalar.copy(out=xT[:, e0 : e0 + ENVS_IN_BANK, :, :], in_=xT_ps[:])

        h1_bf16 = {}
        h1_grouped = {}
        h1_codes = {}
        h1_scales = {}

        def first_layer(e, c):
            h1_bf16[e, c] = h1_pool.tile([P, PACK, BATCH], BF16, name="h1_bf16")
            x_cols = xT[:, e, :, :].rearrange("d s p -> d (s p)")
            for bank in range(PACK // GROUPS_IN_BANK):
                acc = psum_hidden.tile([P, GROUPS_IN_BANK, BATCH], F32, name="hidden_acc")
                for j in range(GROUPS_IN_BANK):
                    chunk = c * PACK + bank * GROUPS_IN_BANK + j
                    nc.tensor.matmul(
                        out=acc[:, j, :],
                        lhsT=w1_sb[:, e, chunk * P : (chunk + 1) * P],
                        rhs=x_cols,
                        start=True,
                        stop=True,
                    )
                for j in range(GROUPS_IN_BANK):
                    chunk = c * PACK + bank * GROUPS_IN_BANK + j
                    nc.scalar.activation(
                        out=h1_bf16[e, c][:, bank * GROUPS_IN_BANK + j, :],
                        in_=acc[:, j, :],
                        func=SILU,
                        bias=bias_cols[:, e * CHUNKS + chunk : e * CHUNKS + chunk + 1],
                    )

        def regroup_h1(e, c):
            h1_grouped[e, c] = h1_pool.tile([P, BATCH, PACK], BF16, name="h1_grouped", align_bytes=64)
            split = BATCH - H1_SCALAR_COLS
            nc.vector.tensor_copy(
                out=h1_grouped[e, c][:, 0:split, :].rearrange("p (k i) t -> p k t i", i=RUN),
                in_=h1_bf16[e, c][:, :, 0:split].rearrange("p t (k i) -> p k t i", i=RUN),
            )
            nc.scalar.copy(
                out=h1_grouped[e, c][:, split:BATCH, :].rearrange("p (k i) t -> p k t i", i=RUN),
                in_=h1_bf16[e, c][:, :, split:BATCH].rearrange("p t (k i) -> p k t i", i=RUN),
            )

        def quantise_h1(e, c):
            if c == 0:
                h1_codes[e] = h1_mx_pool.tile([P, PASSES, BATCH], U32, name="h1_codes", align_bytes=64)
                h1_scales[e] = h1_mx_pool.tile([P, PASSES, BATCH], U8, name="h1_scales", align_bytes=64)
            nc.vector.quantize_mx(
                out=h1_codes[e][:, c, :].bitcast(FP8X4),
                scales=h1_scales[e][:, c, :],
                in_=h1_grouped[e, c][:].rearrange("p w t -> p (w t)"),
            )

        w2_grouped = {}
        w2_codes = {}
        w2_scales = {}

        def regroup_w2(e, half, c0, c1):
            if c0 == 0:
                w2_grouped[e, half] = grouped_pool.tile(
                    [P, PASSES, HALF, PACK], BF16, name="w2_grouped", align_bytes=64
                )
            nc.vector.tensor_copy(
                out=w2_grouped[e, half][:, c0:c1, :, :].rearrange("p c (k i) t -> p c k t i", i=RUN),
                in_=w2_raw[e][:, c0:c1, :, half * HALF : (half + 1) * HALF].rearrange(
                    "p c t (k i) -> p c k t i", i=RUN
                ),
            )

        def quantise_w2(e, half, c0, c1):
            if c0 == 0:
                w2_codes[e, half] = w2_mx_pool.tile([P, PASSES, HALF], U32, name="w2_codes", align_bytes=64)
                w2_scales[e, half] = w2_mx_pool.tile([P, PASSES, HALF], U8, name="w2_scales", align_bytes=64)
            nc.vector.quantize_mx(
                out=w2_codes[e, half][:, c0:c1, :].rearrange("p c w -> p (c w)").bitcast(FP8X4),
                scales=w2_scales[e, half][:, c0:c1, :].rearrange("p c w -> p (c w)"),
                in_=w2_grouped[e, half][:, c0:c1, :, :].rearrange("p c w t -> p (c w t)"),
            )

        h2T = {}
        h2_back = {}

        def second_layer(e, half):
            h2T[e, half] = h2_pool.tile([P, COLS, BATCH], F32, name="h2T")
            for bank in range(COLS // GROUPS_IN_BANK):
                acc = psum_mx.tile([P, GROUPS_IN_BANK, BATCH], F32, name="mx_acc")
                for j in range(GROUPS_IN_BANK):
                    col = bank * GROUPS_IN_BANK + j
                    for c in range(PASSES):
                        nc.tensor.matmul_mx(
                            out=acc[:, j, :],
                            lhsT=w2_codes[e, half][:, c, col * P : (col + 1) * P].bitcast(FP8X4),
                            lhsT_scale=w2_scales[e, half][:, c, col * P : (col + 1) * P],
                            rhs=h1_codes[e][:, c, :].bitcast(FP8X4),
                            rhs_scale=h1_scales[e][:, c, :],
                            start=(c == 0),
                            stop=(c == PASSES - 1),
                        )
                for j in range(GROUPS_IN_BANK):
                    col = bank * GROUPS_IN_BANK + j
                    b2_col = ENVS * CHUNKS + e * CHUNKS + half * COLS + col
                    nc.scalar.activation(
                        out=h2T[e, half][:, col, :],
                        in_=acc[:, j, :],
                        func=SILU,
                        bias=bias_cols[:, b2_col : b2_col + 1],
                    )

        def transpose_back(e, half):
            for s in range(ROW_SETS):
                h2_back[e, half, s] = psum_back.tile([P, COLS, P], F32, name="h2_back")
            for col in range(COLS):
                for s in range(ROW_SETS):
                    nc.tensor.transpose(
                        out=h2_back[e, half, s][:, col, :],
                        in_=h2T[e, half][:, col, s * P : (s + 1) * P],
                        identity=ident_f32[:],
                    )

        out_rows = out.rearrange("(p s) e n -> p s e n", s=ROW_SETS)

        def store(e, half, vector_is_free):
            for s in range(ROW_SETS):
                h2_sb = out_pool.tile([P, HALF], F32, name="h2_sb")
                copy = nc.vector.tensor_copy if vector_is_free and s == ROW_SETS - 1 else nc.scalar.copy
                copy(out=h2_sb[:], in_=h2_back[e, half, s][:].rearrange("p c n -> p (c n)"))
                nc.sync.dma_start(out=out_rows[:, s, e, half * HALF : (half + 1) * HALF], in_=h2_sb[:])

        for c in range(PASSES):
            for half in range(HALVES):
                regroup_w2(0, half, c, c + 1)
            for half in range(HALVES):
                quantise_w2(0, half, c, c + 1)
        load_weights(LOAD_AHEAD)
        transpose_x(0)
        for step in range(FIRST_AHEAD + 1):
            first_layer(*divmod(step, PASSES))
            regroup_h1(*divmod(step, PASSES))
        transpose_x(ENVS_IN_BANK)
        for step in range(FIRST_AHEAD + 1):
            quantise_h1(*divmod(step, PASSES))

        for i in range(1, STEPS + 2):
            if 0 <= i - 2:
                store(*divmod(i - 2, HALVES), vector_is_free=(i >= STEPS))
            if HALVES <= i < STEPS:
                e, half = divmod(i, HALVES)
                regroup_w2(e, half, 0, PASSES)
                if i + 1 < STEPS:
                    regroup_h1(*divmod(i + 1, PASSES))
                quantise_w2(e, half, 0, PASSES)
                if i + 1 < STEPS:
                    quantise_h1(*divmod(i + 1, PASSES))
                if half == HALVES - 1 and e + LOAD_AHEAD < ENVS:
                    load_weights(e + LOAD_AHEAD)
            if i - 1 < STEPS:
                second_layer(*divmod(i - 1, HALVES))
            if i + FIRST_AHEAD < STEPS:
                first_layer(*divmod(i + FIRST_AHEAD, PASSES))
            if i - 1 < STEPS:
                transpose_back(*divmod(i - 1, HALVES))
